import numpy as np
import ml_dtypes


def mxq(x, axis, fmt="e4m3"):
    dtype, down = {"e4m3": (ml_dtypes.float8_e4m3fn, 7), "e5m2": (ml_dtypes.float8_e5m2, 14)}[fmt]
    v = np.moveaxis(np.asarray(x, np.float32).astype(ml_dtypes.bfloat16).astype(np.float64), axis, -1)
    blocks = v.reshape(v.shape[:-1] + (-1, 32))
    amax = np.abs(blocks).max(-1, keepdims=True)
    byte = np.maximum(np.where(amax > 0, np.frexp(amax)[1] - 1 + 127, 0) - down, 1)
    scale = np.exp2(byte - 127.0)
    codes = (blocks / scale).astype(np.float32).astype(dtype).astype(np.float64)
    return np.moveaxis((codes * scale).reshape(v.shape), -1, axis)


WIDE = False


def mx_kscale(k):
    if not WIDE:
        return np.ones(k)
    levels = np.array([10, -10, 5, -5, 0])
    a = np.random.permutation(np.resize(levels, k // 512 * 4)).reshape(k // 512, 4)
    idx = np.arange(k)
    return np.exp2(a[idx // 512, idx % 128 // 32])


BF16 = ml_dtypes.bfloat16


def bf(x):
    return np.asarray(x, np.float32).astype(BF16)


def f64(x):
    return np.asarray(x).astype(np.float64)


B, S, NH, HD = 4, 512, 12, 128
H = NH * HD


def split_heads(x):
    return x.reshape(B, S, NH, HD).transpose(0, 2, 1, 3)


def setup_inputs():
    t = mx_kscale(S)
    t = t / t.max()
    kind = np.random.randint(0, 4, (B, S))
    base = np.where(kind < 2, 0.0, np.where(kind == 2, -10000.0, np.random.standard_normal((B, S))))
    return {"model_hidden_states": bf(np.random.standard_normal((B, S, H))),
            "k_hidden_states": bf(np.random.standard_normal((B, S, H))),
            "k_embeddings": bf(np.random.standard_normal((B, S, H)) * 0.15 * np.sqrt(S) / t[None, :, None]),
            "attention_mask": bf(base + np.log(t)[None, :])}


def reference(model_hidden_states, k_hidden_states, k_embeddings, attention_mask):
    q = split_heads(f64(model_hidden_states))
    k = split_heads(f64(k_hidden_states))
    v = split_heads(f64(k_embeddings))
    energy = q @ k.transpose(0, 1, 3, 2) / np.sqrt(HD)
    m = f64(attention_mask)[:, None, None, :]
    energy = np.where(m == 0, energy, m)
    e = np.exp(energy - energy.max(-1, keepdims=True))
    attn = (mxq(e, 3, "e4m3") @ mxq(v, 2, "e4m3")) / e.sum(-1, keepdims=True)
    return attn.transpose(0, 2, 1, 3).reshape(B, S, H)

@@ -1,0 +1,189 @@
+import math
+from contextlib import ExitStack
+
+import concourse.mybir as mybir
+from concourse.masks import make_identity
+
+B, S, NH, HD = 4, 512, 12, 128
+FLOPS = 2 * 2 * B * NH * S * S * HD
+
+BF16 = mybir.dt.bfloat16
+F32 = mybir.dt.float32
+U32 = mybir.dt.uint32
+U8 = mybir.dt.uint8
+FP8X4 = mybir.dt.float8_e4m3fn_x4
+ALU = mybir.AluOpType
+ACTF = mybir.ActivationFunctionType
+AX = mybir.AxisListType
+
+P = 128
+NT = S // P
+GH = 4
+NG = NH // GH
+GC = GH * HD
+
+
+def tile_knnattention_kernel(tc, model_hidden_states, k_hidden_states, k_embeddings, attention_mask, out):
+    nc = tc.nc
+    scale = 1.0 / math.sqrt(HD)
+    q_dram = model_hidden_states.rearrange("b (p t) c -> b p t c", t=NT)
+    k_dram = k_hidden_states.rearrange("b (p t) c -> b p t c", t=NT)
+    v_dram = k_embeddings.rearrange("b (p t) c -> b p t c", t=NT)
+    o_dram = out.rearrange("b (p t) c -> b p t c", t=NT)
+    with ExitStack() as ctx:
+        const = ctx.enter_context(tc.tile_pool(name="const", bufs=1))
+        loads = ctx.enter_context(tc.tile_pool(name="loads", bufs=3))
+        work = ctx.enter_context(tc.tile_pool(name="work", bufs=3))
+        small = ctx.enter_context(tc.tile_pool(name="small", bufs=6))
+        psum = ctx.enter_context(tc.psum_pool(name="psum", bufs=1))
+
+        mask_bf = const.tile([P, B * S], BF16)
+        nc.sync.dma_start(out=mask_bf[:], in_=attention_mask.rearrange("b s -> (b s)").partition_broadcast(P))
+        ident_bf = const.tile([P, P], BF16)
+        make_identity(nc, ident_bf[:])
+        ident_f = const.tile([P, P], F32)
+        make_identity(nc, ident_f[:])
+
+        groups = {}
+
+        def load_group(n):
+            b, g = divmod(n, NG)
+            cols = slice(g * GC, (g + 1) * GC)
+            q_sb = loads.tile([P, NT, GC], BF16, tag="q")
+            nc.sync.dma_start(out=q_sb[:], in_=q_dram[b, :, :, cols])
+            k_sb = loads.tile([P, NT, GC], BF16, tag="k")
+            nc.sync.dma_start(out=k_sb[:], in_=k_dram[b, :, :, cols])
+            v_sb = loads.tile([P, NT, GC], BF16, tag="v")
+            nc.sync.dma_start(out=v_sb[:], in_=v_dram[b, :, :, cols])
+            groups[n] = {"q": q_sb, "k": k_sb, "v": v_sb}
+
+        def prep_v(n):
+            grp = groups[n]
+            vg = work.tile([P, GC, NT], BF16, tag="vg", bufs=2, align_bytes=64)
+            nc.gpsimd.tensor_scalar(out=vg[:], in0=grp["v"][:].rearrange("p j c -> p c j"),
+                                    scalar1=1.0, scalar2=0.0, op0=ALU.mult, op1=ALU.add)
+            v_codes = work.tile([P, GC], U32, tag="vc", bufs=3, align_bytes=64)
+            v_scales = work.tile([P, GC], U8, tag="vs", bufs=3, align_bytes=64)
+            nc.vector.quantize_mx(out=v_codes[:].bitcast(FP8X4), scales=v_scales[:],
+                                  in_=vg[:].rearrange("p c j -> p (c j)"))
+            grp["vc"] = v_codes
+            grp["vs"] = v_scales
+            o_sb = work.tile([P, NT, GC], F32, tag="o_sb", bufs=2)
+            grp["o"] = o_sb
+
+        load_group(0)
+        load_group(1)
+
+        mask_k = mask_bf[:].rearrange("x (b p j) -> x b j p", b=B, p=P, j=NT)
+        keep = const.tile([P, B, NT, P], BF16)
+        nc.vector.tensor_scalar(out=keep[:], in0=mask_k, scalar1=0.0, scalar2=None, op0=ALU.is_equal)
+        diagk = const.tile([P, B, NT, P], BF16)
+        nc.vector.tensor_tensor(out=diagk[:].rearrange("x b j p -> x (b j) p"),
+                                in0=keep[:].rearrange("x b j p -> x (b j) p"),
+                                in1=ident_bf[:].unsqueeze(1).to_broadcast([P, B * NT, P]), op=ALU.mult)
+        maskc = const.tile([P, B, NT, P], F32)
+        nc.vector.tensor_scalar(out=maskc[:], in0=mask_k, scalar1=math.sqrt(HD), scalar2=None, op0=ALU.mult)
+        mb = const.tile([P, B, NT, P], F32)
+        for b in range(B):
+            mb_ps = psum.tile([P, NT, P], F32, tag="s", bufs=3)
+            for j in range(NT):
+                nc.tensor.transpose(mb_ps[:, j, :], maskc[:, b, j, :], ident_f[:])
+            nc.vector.tensor_copy(out=mb[:, b, :, :], in_=mb_ps[:])
+
+        state = {}
+
+        def where(i):
+            n, hh = divmod(i, GH)
+            return n, n // NG, hh
+
+        def stage_a(i):
+            n, b, hh = where(i)
+            grp = groups[n]
+            hc = slice(hh * HD, (hh + 1) * HD)
+            qk_ps = psum.tile([P, 2 * S], BF16, tag="qk", bufs=2)
+            for t in range(NT):
+                nc.tensor.transpose(qk_ps[:, t * P:(t + 1) * P], grp["q"][:, t, hc], ident_bf[:])
+            for j in range(NT):
+                nc.tensor.transpose(qk_ps[:, S + j * P:S + (j + 1) * P], grp["k"][:, j, hc], diagk[:, b, j, :])
+            qkt = work.tile([P, 2 * S], BF16, tag="qkt", bufs=3)
+            nc.scalar.copy(out=qkt[:], in_=qk_ps[:])
+            state[i] = {"qkt": qkt}
+
+        def stage_b(i):
+            n, b, hh = where(i)
+            st = state[i]
+            qkt = st["qkt"]
+            e_sb = work.tile([P, NT, S], BF16, tag="e", bufs=3)
+            negm = small.tile([P, NT], F32, tag="negm")
+            bias = small.tile([P, NT], F32, tag="bias")
+            rsum = small.tile([P, NT], F32, tag="rsum")
+            for t in range(NT):
+                s_ps = psum.tile([P, S], F32, tag="s", bufs=3)
+                for j in range(NT):
+                    nc.tensor.matmul(out=s_ps[:, j * P:(j + 1) * P], lhsT=mb[:, b, j, :], rhs=ident_f[:],
+                                     is_transpose=True, start=(j == 0), stop=False)
+                nc.tensor.matmul(out=s_ps[:], lhsT=qkt[:, t * P:(t + 1) * P], rhs=qkt[:, S:2 * S],
+                                 start=False, stop=True)
+                nc.vector.tensor_reduce(out=negm[:, t:t + 1], in_=s_ps[:], axis=AX.X, op=ALU.max, negate=True)
+                nc.vector.tensor_scalar(out=bias[:, t:t + 1], in0=negm[:, t:t + 1], scalar1=scale, scalar2=None,
+                                        op0=ALU.mult)
+                nc.scalar.activation(out=e_sb[:, t, :], in_=s_ps[:], func=ACTF.Exp, bias=bias[:, t:t + 1],
+                                     scale=scale, accum_out=rsum[:, t:t + 1])
+            st["e"] = e_sb
+            st["rsum"] = rsum
+
+        def stage_c(i):
+            st = state[i]
+            e_sb = st["e"]
+            eg = work.tile([P, NT, P, NT], BF16, tag="eg", bufs=3, align_bytes=64)
+            for half in range(2):
+                et_ps = psum.tile([P, 2, NT, P], BF16, tag="et", bufs=2)
+                for tt in range(2):
+                    for j in range(NT):
+                        nc.tensor.transpose(et_ps[:, tt, j, :], e_sb[:, 2 * half + tt, j * P:(j + 1) * P], ident_bf[:])
+                et_sb = work.tile([P, 2, NT, P], BF16, tag="et_sb", bufs=3)
+                nc.scalar.copy(out=et_sb[:], in_=et_ps[:])
+                nc.gpsimd.tensor_scalar(out=eg[:, 2 * half:2 * half + 2, :, :],
+                                        in0=et_sb[:].rearrange("p t j q -> p t q j"),
+                                        scalar1=1.0, scalar2=0.0, op0=ALU.mult, op1=ALU.add)
+            e_codes = work.tile([P, S], U32, tag="ec", bufs=3, align_bytes=64)
+            e_scales = work.tile([P, S], U8, tag="es", bufs=3, align_bytes=64)
+            nc.vector.quantize_mx(out=e_codes[:].bitcast(FP8X4), scales=e_scales[:],
+                                  in_=eg[:].rearrange("p t q j -> p (t q j)"))
+            st["ec"] = e_codes
+            st["es"] = e_scales
+
+        def stage_d(i):
+            n, b, hh = where(i)
+            grp = groups[n]
+            st = state[i]
+            hc = slice(hh * HD, (hh + 1) * HD)
+            o_ps = psum.tile([P, NT, HD], F32, tag="o", bufs=1)
+            for t in range(NT):
+                tq = slice(t * P, (t + 1) * P)
+                nc.tensor.matmul_mx(out=o_ps[:, t, :], lhsT=st["ec"][:, tq].bitcast(FP8X4), lhsT_scale=st["es"][:, tq],
+                                    rhs=grp["vc"][:, hc].bitcast(FP8X4), rhs_scale=grp["vs"][:, hc],
+                                    start=True, stop=True)
+            recip = small.tile([P, NT], F32, tag="recip")
+            nc.vector.reciprocal(out=recip[:], in_=st["rsum"][:])
+            nc.vector.tensor_tensor(out=grp["o"][:, :, hc], in0=o_ps[:],
+                                    in1=recip[:].unsqueeze(2).to_broadcast([P, NT, HD]), op=ALU.mult)
+            if hh == GH - 1:
+                g = n % NG
+                nc.sync.dma_start(out=o_dram[b, :, :, g * GC:(g + 1) * GC], in_=grp["o"][:])
+
+        total = B * NH
+        for step in range(total + 3):
+            if step < total:
+                n, hh = divmod(step, GH)
+                if hh == 0:
+                    prep_v(n)
+                    if n + 2 < B * NG:
+                        load_group(n + 2)
+                stage_a(step)
+            if 1 <= step < total + 1:
+                stage_b(step - 1)
+            if 2 <= step < total + 2:
+                stage_c(step - 2)
+            if 3 <= step:
+                stage_d(step - 3)

@@ -14,13 +14,15 @@ U8 = mybir.dt.uint8
 FP8X4 = mybir.dt.float8_e4m3fn_x4
 ALU = mybir.AluOpType
 ACTF = mybir.ActivationFunctionType
-AX = mybir.AxisListType
 
 P = 128
 NT = S // P
 GH = 4
 NG = NH // GH
 GC = GH * HD
+HEADS = B * NH
+TILES = HEADS * NT
+LEAD = 6
 
 
 def tile_knnattention_kernel(tc, model_hidden_states, k_hidden_states, k_embeddings, attention_mask, out):
@@ -36,18 +38,21 @@ def tile_knnattention_kernel(tc, model_hidden_states, k_hidden_states, k_embeddi
         work = ctx.enter_context(tc.tile_pool(name="work", bufs=3))
         small = ctx.enter_context(tc.tile_pool(name="small", bufs=6))
         psum = ctx.enter_context(tc.psum_pool(name="psum", bufs=1))
-
-        mask_bf = const.tile([P, B * S], BF16)
-        nc.sync.dma_start(out=mask_bf[:], in_=attention_mask.rearrange("b s -> (b s)").partition_broadcast(P))
-        ident_bf = const.tile([P, P], BF16)
-        make_identity(nc, ident_bf[:])
-        ident_f = const.tile([P, P], F32)
-        make_identity(nc, ident_f[:])
+        ctx.enter_context(tc.manual_schedule())
 
         groups = {}
+        batch = {}
+        heads = {}
+        pairs = {}
+        tiles = {}
 
-        def load_group(n):
-            b, g = divmod(n, NG)
+        def load_mask(b):
+            mask_bf = const.tile([P, S], BF16, name="mask%d" % b)
+            nc.sync.dma_start(out=mask_bf[:], in_=attention_mask[b, :].partition_broadcast(P))
+            batch[b] = {"mask": mask_bf}
+
+        def load_group(m):
+            b, g = divmod(m, NG)
             cols = slice(g * GC, (g + 1) * GC)
             q_sb = loads.tile([P, NT, GC], BF16, tag="q")
             nc.sync.dma_start(out=q_sb[:], in_=q_dram[b, :, :, cols])
@@ -55,135 +60,223 @@ def tile_knnattention_kernel(tc, model_hidden_states, k_hidden_states, k_embeddi
             nc.sync.dma_start(out=k_sb[:], in_=k_dram[b, :, :, cols])
             v_sb = loads.tile([P, NT, GC], BF16, tag="v")
             nc.sync.dma_start(out=v_sb[:], in_=v_dram[b, :, :, cols])
-            groups[n] = {"q": q_sb, "k": k_sb, "v": v_sb}
+            groups[m] = {"q": q_sb, "k": k_sb, "v": v_sb}
 
-        def prep_v(n):
-            grp = groups[n]
-            vg = work.tile([P, GC, NT], BF16, tag="vg", bufs=2, align_bytes=64)
-            nc.gpsimd.tensor_scalar(out=vg[:], in0=grp["v"][:].rearrange("p j c -> p c j"),
-                                    scalar1=1.0, scalar2=0.0, op0=ALU.mult, op1=ALU.add)
-            v_codes = work.tile([P, GC], U32, tag="vc", bufs=3, align_bytes=64)
-            v_scales = work.tile([P, GC], U8, tag="vs", bufs=3, align_bytes=64)
-            nc.vector.quantize_mx(out=v_codes[:].bitcast(FP8X4), scales=v_scales[:],
-                                  in_=vg[:].rearrange("p c j -> p (c j)"))
-            grp["vc"] = v_codes
-            grp["vs"] = v_scales
-            o_sb = work.tile([P, NT, GC], F32, tag="o_sb", bufs=2)
-            grp["o"] = o_sb
+        def setup_keep(b):
+            mask_k = batch[b]["mask"][:].rearrange("x (p j) -> x j p", j=NT)
+            keep = const.tile([P, NT, P], BF16, name="keep%d" % b)
+            nc.vector.tensor_scalar(out=keep[:], in0=mask_k, scalar1=0.0, scalar2=None, op0=ALU.is_equal)
+            diagk = const.tile([P, NT, P], BF16, name="diagk%d" % b)
+            nc.vector.tensor_tensor(out=diagk[:], in0=keep[:],
+                                    in1=ident_bf[:].unsqueeze(1).to_broadcast([P, NT, P]), op=ALU.mult)
+            batch[b]["diagk"] = diagk
 
-        load_group(0)
-        load_group(1)
+        def setup_maskc(b):
+            mask_k = batch[b]["mask"][:].rearrange("x (p j) -> x j p", j=NT)
+            maskc = const.tile([P, NT, P], F32, name="maskc%d" % b)
+            nc.vector.tensor_scalar(out=maskc[:], in0=mask_k, scalar1=math.sqrt(HD), scalar2=None, op0=ALU.mult)
+            batch[b]["maskc"] = maskc
 
-        mask_k = mask_bf[:].rearrange("x (b p j) -> x b j p", b=B, p=P, j=NT)
-        keep = const.tile([P, B, NT, P], BF16)
-        nc.vector.tensor_scalar(out=keep[:], in0=mask_k, scalar1=0.0, scalar2=None, op0=ALU.is_equal)
-        diagk = const.tile([P, B, NT, P], BF16)
-        nc.vector.tensor_tensor(out=diagk[:].rearrange("x b j p -> x (b j) p"),
-                                in0=keep[:].rearrange("x b j p -> x (b j) p"),
-                                in1=ident_bf[:].unsqueeze(1).to_broadcast([P, B * NT, P]), op=ALU.mult)
-        maskc = const.tile([P, B, NT, P], F32)
-        nc.vector.tensor_scalar(out=maskc[:], in0=mask_k, scalar1=math.sqrt(HD), scalar2=None, op0=ALU.mult)
-        mb = const.tile([P, B, NT, P], F32)
-        for b in range(B):
+        def setup_mb_pe(b):
             mb_ps = psum.tile([P, NT, P], F32, tag="s", bufs=3)
             for j in range(NT):
-                nc.tensor.transpose(mb_ps[:, j, :], maskc[:, b, j, :], ident_f[:])
-            nc.vector.tensor_copy(out=mb[:, b, :, :], in_=mb_ps[:])
+                nc.tensor.transpose(mb_ps[:, j, :], batch[b]["maskc"][:, j, :], ident_f[:])
+            batch[b]["mb_ps"] = mb_ps
 
-        state = {}
+        def setup_mb_copy(b):
+            mb = const.tile([P, NT, P], F32, name="mb%d" % b)
+            nc.vector.tensor_copy(out=mb[:], in_=batch[b]["mb_ps"][:])
+            batch[b]["mb"] = mb
 
         def where(i):
-            n, hh = divmod(i, GH)
-            return n, n // NG, hh
+            m, hh = divmod(i, GH)
+            return m, m // NG, hh
 
-        def stage_a(i):
-            n, b, hh = where(i)
-            grp = groups[n]
+        def pe_qk_transposes(i, part):
+            m, b, hh = where(i)
+            grp = groups[m]
             hc = slice(hh * HD, (hh + 1) * HD)
-            qk_ps = psum.tile([P, 2 * S], BF16, tag="qk", bufs=2)
-            for t in range(NT):
-                nc.tensor.transpose(qk_ps[:, t * P:(t + 1) * P], grp["q"][:, t, hc], ident_bf[:])
-            for j in range(NT):
-                nc.tensor.transpose(qk_ps[:, S + j * P:S + (j + 1) * P], grp["k"][:, j, hc], diagk[:, b, j, :])
+            if part == 0:
+                qk_ps = psum.tile([P, 2 * S], BF16, tag="qk", bufs=1)
+                heads[i] = {"qk_ps": qk_ps}
+            qk_ps = heads[i]["qk_ps"]
+            for x in ((0, 1, 2), (3, 4, 5), (6, 7))[part]:
+                if x < NT:
+                    nc.tensor.transpose(qk_ps[:, x * P:(x + 1) * P], grp["q"][:, x, hc], ident_bf[:])
+                else:
+                    nc.tensor.transpose(qk_ps[:, x * P:(x + 1) * P], grp["k"][:, x - NT, hc],
+                                        batch[b]["diagk"][:, x - NT, :])
+
+        def act_qk_copy(i):
             qkt = work.tile([P, 2 * S], BF16, tag="qkt", bufs=3)
-            nc.scalar.copy(out=qkt[:], in_=qk_ps[:])
-            state[i] = {"qkt": qkt}
+            nc.scalar.copy(out=qkt[:], in_=heads[i]["qk_ps"][:])
+            heads[i]["qkt"] = qkt
 
-        def stage_b(i):
-            n, b, hh = where(i)
-            st = state[i]
-            qkt = st["qkt"]
-            e_sb = work.tile([P, NT, S], BF16, tag="e", bufs=3)
-            negm = small.tile([P, NT], F32, tag="negm")
-            bias = small.tile([P, NT], F32, tag="bias")
-            rsum = small.tile([P, NT], F32, tag="rsum")
-            for t in range(NT):
-                s_ps = psum.tile([P, S], F32, tag="s", bufs=3)
-                for j in range(NT):
-                    nc.tensor.matmul(out=s_ps[:, j * P:(j + 1) * P], lhsT=mb[:, b, j, :], rhs=ident_f[:],
-                                     is_transpose=True, start=(j == 0), stop=False)
-                nc.tensor.matmul(out=s_ps[:], lhsT=qkt[:, t * P:(t + 1) * P], rhs=qkt[:, S:2 * S],
-                                 start=False, stop=True)
-                nc.vector.tensor_reduce(out=negm[:, t:t + 1], in_=s_ps[:], axis=AX.X, op=ALU.max, negate=True)
-                nc.vector.tensor_scalar(out=bias[:, t:t + 1], in0=negm[:, t:t + 1], scalar1=scale, scalar2=None,
-                                        op0=ALU.mult)
-                nc.scalar.activation(out=e_sb[:, t, :], in_=s_ps[:], func=ACTF.Exp, bias=bias[:, t:t + 1],
-                                     scale=scale, accum_out=rsum[:, t:t + 1])
-            st["e"] = e_sb
-            st["rsum"] = rsum
+        def pe_scores(n):
+            i, t = divmod(n, NT)
+            m, b, hh = where(i)
+            qkt = heads[i]["qkt"]
+            mb = batch[b]["mb"]
+            s_ps = psum.tile([P, S], F32, tag="s", bufs=3)
+            for j in range(NT):
+                nc.tensor.matmul(out=s_ps[:, j * P:(j + 1) * P], lhsT=mb[:, j, :], rhs=ident_f[:],
+                                 is_transpose=True, start=(j == 0), stop=False)
+            nc.tensor.matmul(out=s_ps[:], lhsT=qkt[:, t * P:(t + 1) * P], rhs=qkt[:, S:2 * S],
+                             start=False, stop=True)
+            tiles[n] = {"s": s_ps}
 
-        def stage_c(i):
-            st = state[i]
-            e_sb = st["e"]
-            eg = work.tile([P, NT, P, NT], BF16, tag="eg", bufs=3, align_bytes=64)
-            for half in range(2):
-                et_ps = psum.tile([P, 2, NT, P], BF16, tag="et", bufs=2)
-                for tt in range(2):
-                    for j in range(NT):
-                        nc.tensor.transpose(et_ps[:, tt, j, :], e_sb[:, 2 * half + tt, j * P:(j + 1) * P], ident_bf[:])
+        def dve_max(n):
+            i, t = divmod(n, NT)
+            if t == 0:
+                bias = small.tile([P, NT], F32, tag="bias")
+                heads[i]["bias"] = bias
+            y_sb = work.tile([P, S], F32, tag="y", bufs=4)
+            nc.vector.tensor_scalar(out=y_sb[:], in0=tiles[n]["s"][:], scalar1=-scale, scalar2=None, op0=ALU.mult,
+                                    op1=ALU.min, accum_out=heads[i]["bias"][:, t:t + 1])
+            tiles[n]["y"] = y_sb
+
+        def act_exp(n):
+            i, t = divmod(n, NT)
+            if t == 0:
+                rsum = small.tile([P, NT], F32, tag="rsum")
+                heads[i]["rsum"] = rsum
+            e_sb = work.tile([P, S], BF16, tag="e", bufs=4)
+            nc.scalar.activation(out=e_sb[:], in_=tiles[n]["y"][:], func=ACTF.Exp, bias=heads[i]["bias"][:, t:t + 1],
+                                 scale=-1.0, accum_out=heads[i]["rsum"][:, t:t + 1])
+            tiles[n]["e"] = e_sb
+
+        def pe_e_transposes(n):
+            et_ps = psum.tile([P, NT, P], BF16, tag="et", bufs=3)
+            for j in range(NT):
+                nc.tensor.transpose(et_ps[:, j, :], tiles[n]["e"][:, j * P:(j + 1) * P], ident_bf[:])
+            tiles[n]["et"] = et_ps
+
+        def act_e_copy(n):
+            mp, tt = divmod(n, 2)
+            if tt == 0:
                 et_sb = work.tile([P, 2, NT, P], BF16, tag="et_sb", bufs=3)
-                nc.scalar.copy(out=et_sb[:], in_=et_ps[:])
-                nc.gpsimd.tensor_scalar(out=eg[:, 2 * half:2 * half + 2, :, :],
-                                        in0=et_sb[:].rearrange("p t j q -> p t q j"),
-                                        scalar1=1.0, scalar2=0.0, op0=ALU.mult, op1=ALU.add)
-            e_codes = work.tile([P, S], U32, tag="ec", bufs=3, align_bytes=64)
-            e_scales = work.tile([P, S], U8, tag="es", bufs=3, align_bytes=64)
-            nc.vector.quantize_mx(out=e_codes[:].bitcast(FP8X4), scales=e_scales[:],
-                                  in_=eg[:].rearrange("p t q j -> p (t q j)"))
-            st["ec"] = e_codes
-            st["es"] = e_scales
+                pairs[mp] = {"et_sb": et_sb}
+            nc.scalar.copy(out=pairs[mp]["et_sb"][:, tt, :, :], in_=tiles[n]["et"][:])
 
-        def stage_d(i):
-            n, b, hh = where(i)
-            grp = groups[n]
-            st = state[i]
+        def pool_regroup(mp):
+            eg = work.tile([P, 2, P, NT], BF16, tag="eg", bufs=3, align_bytes=64)
+            nc.gpsimd.tensor_scalar(out=eg[:], in0=pairs[mp]["et_sb"][:].rearrange("p t j q -> p t q j"),
+                                    scalar1=1.0, scalar2=0.0, op0=ALU.mult, op1=ALU.add)
+            pairs[mp]["eg"] = eg
+
+        def dve_quant(mp):
+            e_codes = work.tile([P, 2 * P], U32, tag="ec", bufs=4, align_bytes=64)
+            e_scales = work.tile([P, 2 * P], U8, tag="es", bufs=4, align_bytes=64)
+            nc.vector.quantize_mx(out=e_codes[:].bitcast(FP8X4), scales=e_scales[:],
+                                  in_=pairs[mp]["eg"][:].rearrange("p t q j -> p (t q j)"))
+            pairs[mp]["ec"] = e_codes
+            pairs[mp]["es"] = e_scales
+
+        def dve_v_regroup(i):
+            m, b, hh = where(i)
+            hc = slice(hh * HD, (hh + 1) * HD)
+            vg = work.tile([P, HD, NT], BF16, tag="vg", bufs=2, align_bytes=64)
+            nc.vector.tensor_copy(out=vg[:].rearrange("p (c x) j -> p c j x", x=4),
+                                  in_=groups[m]["v"][:, :, hc].rearrange("p j (c x) -> p c j x", x=4))
+            heads[i]["vg"] = vg
+
+        def dve_v_quant(i):
+            m, b, hh = where(i)
+            hc = slice(hh * HD, (hh + 1) * HD)
+            if hh == 0:
+                v_codes = work.tile([P, GC], U32, tag="vc", bufs=3, align_bytes=64)
+                v_scales = work.tile([P, GC], U8, tag="vs", bufs=3, align_bytes=64)
+                groups[m]["vc"] = v_codes
+                groups[m]["vs"] = v_scales
+            nc.vector.quantize_mx(out=groups[m]["vc"][:, hc].bitcast(FP8X4), scales=groups[m]["vs"][:, hc],
+                                  in_=heads[i]["vg"][:].rearrange("p c j -> p (c j)"))
+
+        def pe_pv(i):
+            m, b, hh = where(i)
+            grp = groups[m]
             hc = slice(hh * HD, (hh + 1) * HD)
             o_ps = psum.tile([P, NT, HD], F32, tag="o", bufs=1)
             for t in range(NT):
-                tq = slice(t * P, (t + 1) * P)
-                nc.tensor.matmul_mx(out=o_ps[:, t, :], lhsT=st["ec"][:, tq].bitcast(FP8X4), lhsT_scale=st["es"][:, tq],
+                pr = pairs[(i * NT + t) // 2]
+                tq = slice((t % 2) * P, (t % 2 + 1) * P)
+                nc.tensor.matmul_mx(out=o_ps[:, t, :], lhsT=pr["ec"][:, tq].bitcast(FP8X4), lhsT_scale=pr["es"][:, tq],
                                     rhs=grp["vc"][:, hc].bitcast(FP8X4), rhs_scale=grp["vs"][:, hc],
                                     start=True, stop=True)
-            recip = small.tile([P, NT], F32, tag="recip")
-            nc.vector.reciprocal(out=recip[:], in_=st["rsum"][:])
-            nc.vector.tensor_tensor(out=grp["o"][:, :, hc], in0=o_ps[:],
-                                    in1=recip[:].unsqueeze(2).to_broadcast([P, NT, HD]), op=ALU.mult)
-            if hh == GH - 1:
-                g = n % NG
+            heads[i]["o_ps"] = o_ps
+
+        def dve_out(i, half):
+            m, b, hh = where(i)
+            grp = groups[m]
+            hc = slice(hh * HD, (hh + 1) * HD)
+            if half == 0:
+                if hh == 0:
+                    o_sb = work.tile([P, NT, GC], F32, tag="o_sb", bufs=2)
+                    grp["o"] = o_sb
+                recip = small.tile([P, NT], F32, tag="recip")
+                nc.vector.reciprocal(out=recip[:], in_=heads[i]["rsum"][:])
+                heads[i]["recip"] = recip
+            th = slice(2 * half, 2 * half + 2)
+            nc.vector.tensor_tensor(out=grp["o"][:, th, hc], in0=heads[i]["o_ps"][:, th, :],
+                                    in1=heads[i]["recip"][:, th].unsqueeze(2).to_broadcast([P, 2, HD]), op=ALU.mult)
+            if half == 1 and hh == GH - 1:
+                g = m % NG
                 nc.sync.dma_start(out=o_dram[b, :, :, g * GC:(g + 1) * GC], in_=grp["o"][:])
 
-        total = B * NH
-        for step in range(total + 3):
-            if step < total:
-                n, hh = divmod(step, GH)
-                if hh == 0:
-                    prep_v(n)
-                    if n + 2 < B * NG:
-                        load_group(n + 2)
-                stage_a(step)
-            if 1 <= step < total + 1:
-                stage_b(step - 1)
-            if 2 <= step < total + 2:
-                stage_c(step - 2)
-            if 3 <= step:
-                stage_d(step - 3)
+        load_mask(0)
+        load_group(0)
+        for b in range(1, B):
+            load_mask(b)
+        load_group(1)
+        load_group(2)
+        ident_bf = const.tile([P, P], BF16)
+        make_identity(nc, ident_bf[:])
+        ident_f = const.tile([P, P], F32)
+        make_identity(nc, ident_f[:])
+        setup_keep(0)
+        setup_maskc(0)
+        setup_mb_pe(0)
+        setup_mb_copy(0)
+
+        for s in range(TILES + LEAD + 13):
+            x = s - LEAD
+            if 0 <= x - 3 < TILES:
+                pe_e_transposes(x - 3)
+            if 0 <= x < TILES:
+                pe_scores(x)
+            i, r = divmod(s, NT)
+            if i < HEADS and r < 3:
+                pe_qk_transposes(i, r)
+            if x >= 10 and (x - 10) % NT == 0 and (x - 10) // NT < HEADS:
+                pe_pv((x - 10) // NT)
+            if 0 <= x - 1 < TILES:
+                dve_max(x - 1)
+            if x >= 7 and (x - 7) % 2 == 0 and (x - 7) // 2 < TILES // 2:
+                dve_quant((x - 7) // 2)
+            if x >= 11 and (x - 11) % NT == 0 and (x - 11) // NT < HEADS:
+                dve_out((x - 11) // NT, 0)
+            if x >= 12 and (x - 12) % NT == 0 and (x - 12) // NT < HEADS:
+                dve_out((x - 12) // NT, 1)
+            if x >= 2 and (x - 2) % NT == 0 and (x - 2) // NT < HEADS:
+                dve_v_regroup((x - 2) // NT)
+            if x >= 4 and (x - 4) % NT == 0 and (x - 4) // NT < HEADS:
+                dve_v_quant((x - 4) // NT)
+            if 0 <= x - 2 < TILES:
+                act_exp(x - 2)
+            if 0 <= x - 4 < TILES:
+                act_e_copy(x - 4)
+            if i < HEADS and r == 3:
+                act_qk_copy(i)
+            if x >= 6 and (x - 6) % 2 == 0 and (x - 6) // 2 < TILES // 2:
+                pool_regroup((x - 6) // 2)
+            if s >= 22 and (s - 22) % (GH * NT) == 0 and (s - 22) // (GH * NT) + 3 < B * NG:
+                load_group((s - 22) // (GH * NT) + 3)
+            for b in range(1, B):
+                base = NH * NT * (b - 1) + LEAD + 20
+                if s == base:
+                    setup_keep(b)
+                if s == base + 1:
+                    setup_maskc(b)
+                if s == base + 2:
+                    setup_mb_pe(b)
+                if s == base + 3:
+                    setup_mb_copy(b)

@@ -146,17 +146,17 @@ def tile_knnattention_kernel(tc, model_hidden_states, k_hidden_states, k_embeddi
             tiles[n]["e"] = e_sb
 
         def pe_e_transposes(n):
-            et_ps = psum.tile([P, NT, P], BF16, tag="et", bufs=3)
-            for j in range(NT):
-                nc.tensor.transpose(et_ps[:, j, :], tiles[n]["e"][:, j * P:(j + 1) * P], ident_bf[:])
-            tiles[n]["et"] = et_ps
-
-        def act_e_copy(n):
             mp, tt = divmod(n, 2)
             if tt == 0:
-                et_sb = work.tile([P, 2, NT, P], BF16, tag="et_sb", bufs=3)
-                pairs[mp] = {"et_sb": et_sb}
-            nc.scalar.copy(out=pairs[mp]["et_sb"][:, tt, :, :], in_=tiles[n]["et"][:])
+                et_ps = psum.tile([P, 2, NT, P], BF16, tag="et", bufs=3)
+                pairs[mp] = {"et_ps": et_ps}
+            for j in range(NT):
+                nc.tensor.transpose(pairs[mp]["et_ps"][:, tt, j, :], tiles[n]["e"][:, j * P:(j + 1) * P], ident_bf[:])
+
+        def dve_e_copy(mp):
+            et_sb = work.tile([P, 2, NT, P], BF16, tag="et_sb", bufs=3)
+            nc.vector.tensor_copy(out=et_sb[:], in_=pairs[mp]["et_ps"][:])
+            pairs[mp]["et_sb"] = et_sb
 
         def pool_regroup(mp):
             eg = work.tile([P, 2, P, NT], BF16, tag="eg", bufs=3, align_bytes=64)
@@ -172,12 +172,12 @@ def tile_knnattention_kernel(tc, model_hidden_states, k_hidden_states, k_embeddi
             pairs[mp]["ec"] = e_codes
             pairs[mp]["es"] = e_scales
 
-        def dve_v_regroup(i):
+        def pool_v_regroup(i):
             m, b, hh = where(i)
             hc = slice(hh * HD, (hh + 1) * HD)
             vg = work.tile([P, HD, NT], BF16, tag="vg", bufs=2, align_bytes=64)
-            nc.vector.tensor_copy(out=vg[:].rearrange("p (c x) j -> p c j x", x=4),
-                                  in_=groups[m]["v"][:, :, hc].rearrange("p j (c x) -> p c j x", x=4))
+            nc.gpsimd.tensor_scalar(out=vg[:], in0=groups[m]["v"][:, :, hc].rearrange("p j c -> p c j"),
+                                    scalar1=1.0, scalar2=0.0, op0=ALU.mult, op1=ALU.add)
             heads[i]["vg"] = vg
 
         def dve_v_quant(i):
@@ -237,7 +237,7 @@ def tile_knnattention_kernel(tc, model_hidden_states, k_hidden_states, k_embeddi
         setup_mb_pe(0)
         setup_mb_copy(0)
 
-        for s in range(TILES + LEAD + 13):
+        for s in range(TILES + LEAD + 15):
             x = s - LEAD
             if 0 <= x - 3 < TILES:
                 pe_e_transposes(x - 3)
@@ -246,28 +246,28 @@ def tile_knnattention_kernel(tc, model_hidden_states, k_hidden_states, k_embeddi
             i, r = divmod(s, NT)
             if i < HEADS and r < 3:
                 pe_qk_transposes(i, r)
-            if x >= 10 and (x - 10) % NT == 0 and (x - 10) // NT < HEADS:
-                pe_pv((x - 10) // NT)
+            if x >= 11 and (x - 11) % NT == 0 and (x - 11) // NT < HEADS:
+                pe_pv((x - 11) // NT)
             if 0 <= x - 1 < TILES:
                 dve_max(x - 1)
-            if x >= 7 and (x - 7) % 2 == 0 and (x - 7) // 2 < TILES // 2:
-                dve_quant((x - 7) // 2)
-            if x >= 11 and (x - 11) % NT == 0 and (x - 11) // NT < HEADS:
-                dve_out((x - 11) // NT, 0)
+            if x >= 5 and (x - 5) % 2 == 0 and (x - 5) // 2 < TILES // 2:
+                dve_e_copy((x - 5) // 2)
+            if x >= 8 and (x - 8) % 2 == 0 and (x - 8) // 2 < TILES // 2:
+                dve_quant((x - 8) // 2)
             if x >= 12 and (x - 12) % NT == 0 and (x - 12) // NT < HEADS:
-                dve_out((x - 12) // NT, 1)
-            if x >= 2 and (x - 2) % NT == 0 and (x - 2) // NT < HEADS:
-                dve_v_regroup((x - 2) // NT)
-            if x >= 4 and (x - 4) % NT == 0 and (x - 4) // NT < HEADS:
-                dve_v_quant((x - 4) // NT)
+                dve_out((x - 12) // NT, 0)
+            if x >= 14 and (x - 14) % NT == 0 and (x - 14) // NT < HEADS:
+                dve_out((x - 14) // NT, 1)
+            if x >= 5 and (x - 5) % NT == 0 and (x - 5) // NT < HEADS:
+                dve_v_quant((x - 5) // NT)
             if 0 <= x - 2 < TILES:
                 act_exp(x - 2)
-            if 0 <= x - 4 < TILES:
-                act_e_copy(x - 4)
             if i < HEADS and r == 3:
                 act_qk_copy(i)
             if x >= 6 and (x - 6) % 2 == 0 and (x - 6) // 2 < TILES // 2:
                 pool_regroup((x - 6) // 2)
+            if x >= 1 and (x - 1) % NT == 0 and (x - 1) // NT < HEADS:
+                pool_v_regroup((x - 1) // NT)
             if s >= 22 and (s - 22) % (GH * NT) == 0 and (s - 22) // (GH * NT) + 3 < B * NG:
                 load_group((s - 22) // (GH * NT) + 3)
             for b in range(1, B):

@@ -153,43 +153,43 @@ def tile_knnattention_kernel(tc, model_hidden_states, k_hidden_states, k_embeddi
             for j in range(NT):
                 nc.tensor.transpose(pairs[mp]["et_ps"][:, tt, j, :], tiles[n]["e"][:, j * P:(j + 1) * P], ident_bf[:])
 
-        def dve_e_copy(mp):
+        def act_e_copy(mp):
             et_sb = work.tile([P, 2, NT, P], BF16, tag="et_sb", bufs=3)
-            nc.vector.tensor_copy(out=et_sb[:], in_=pairs[mp]["et_ps"][:])
+            nc.scalar.copy(out=et_sb[:], in_=pairs[mp]["et_ps"][:])
             pairs[mp]["et_sb"] = et_sb
 
         def pool_regroup(mp):
-            eg = work.tile([P, 2, P, NT], BF16, tag="eg", bufs=3, align_bytes=64)
-            nc.gpsimd.tensor_scalar(out=eg[:], in0=pairs[mp]["et_sb"][:].rearrange("p t j q -> p t q j"),
+            i, half = divmod(mp, 2)
+            if half == 0:
+                eg = work.tile([P, NT, P, NT], BF16, tag="eg", bufs=3, align_bytes=64)
+                heads[i]["eg"] = eg
+            nc.gpsimd.tensor_scalar(out=heads[i]["eg"][:, 2 * half:2 * half + 2, :, :],
+                                    in0=pairs[mp]["et_sb"][:].rearrange("p t j q -> p t q j"),
                                     scalar1=1.0, scalar2=0.0, op0=ALU.mult, op1=ALU.add)
-            pairs[mp]["eg"] = eg
 
-        def dve_quant(mp):
-            e_codes = work.tile([P, 2 * P], U32, tag="ec", bufs=4, align_bytes=64)
-            e_scales = work.tile([P, 2 * P], U8, tag="es", bufs=4, align_bytes=64)
+        def dve_quant(i):
+            e_codes = work.tile([P, S], U32, tag="ec", bufs=3, align_bytes=64)
+            e_scales = work.tile([P, S], U8, tag="es", bufs=3, align_bytes=64)
             nc.vector.quantize_mx(out=e_codes[:].bitcast(FP8X4), scales=e_scales[:],
-                                  in_=pairs[mp]["eg"][:].rearrange("p t q j -> p (t q j)"))
-            pairs[mp]["ec"] = e_codes
-            pairs[mp]["es"] = e_scales
+                                  in_=heads[i]["eg"][:].rearrange("p t q j -> p (t q j)"))
+            heads[i]["ec"] = e_codes
+            heads[i]["es"] = e_scales
 
-        def pool_v_regroup(i):
-            m, b, hh = where(i)
-            hc = slice(hh * HD, (hh + 1) * HD)
-            vg = work.tile([P, HD, NT], BF16, tag="vg", bufs=2, align_bytes=64)
-            nc.gpsimd.tensor_scalar(out=vg[:], in0=groups[m]["v"][:, :, hc].rearrange("p j c -> p c j"),
-                                    scalar1=1.0, scalar2=0.0, op0=ALU.mult, op1=ALU.add)
-            heads[i]["vg"] = vg
-
-        def dve_v_quant(i):
-            m, b, hh = where(i)
+        def pool_v_regroup(m, hh):
             hc = slice(hh * HD, (hh + 1) * HD)
             if hh == 0:
-                v_codes = work.tile([P, GC], U32, tag="vc", bufs=3, align_bytes=64)
-                v_scales = work.tile([P, GC], U8, tag="vs", bufs=3, align_bytes=64)
-                groups[m]["vc"] = v_codes
-                groups[m]["vs"] = v_scales
-            nc.vector.quantize_mx(out=groups[m]["vc"][:, hc].bitcast(FP8X4), scales=groups[m]["vs"][:, hc],
-                                  in_=heads[i]["vg"][:].rearrange("p c j -> p (c j)"))
+                vg = work.tile([P, GC, NT], BF16, tag="vg", bufs=2, align_bytes=64)
+                groups[m]["vg"] = vg
+            nc.gpsimd.tensor_scalar(out=groups[m]["vg"][:, hc, :], in0=groups[m]["v"][:, :, hc].rearrange("p j c -> p c j"),
+                                    scalar1=1.0, scalar2=0.0, op0=ALU.mult, op1=ALU.add)
+
+        def dve_v_quant(m):
+            v_codes = work.tile([P, GC], U32, tag="vc", bufs=3, align_bytes=64)
+            v_scales = work.tile([P, GC], U8, tag="vs", bufs=3, align_bytes=64)
+            nc.vector.quantize_mx(out=v_codes[:].bitcast(FP8X4), scales=v_scales[:],
+                                  in_=groups[m]["vg"][:].rearrange("p c j -> p (c j)"))
+            groups[m]["vc"] = v_codes
+            groups[m]["vs"] = v_scales
 
         def pe_pv(i):
             m, b, hh = where(i)
@@ -197,28 +197,28 @@ def tile_knnattention_kernel(tc, model_hidden_states, k_hidden_states, k_embeddi
             hc = slice(hh * HD, (hh + 1) * HD)
             o_ps = psum.tile([P, NT, HD], F32, tag="o", bufs=1)
             for t in range(NT):
-                pr = pairs[(i * NT + t) // 2]
-                tq = slice((t % 2) * P, (t % 2 + 1) * P)
+                pr = heads[i]
+                tq = slice(t * P, (t + 1) * P)
                 nc.tensor.matmul_mx(out=o_ps[:, t, :], lhsT=pr["ec"][:, tq].bitcast(FP8X4), lhsT_scale=pr["es"][:, tq],
                                     rhs=grp["vc"][:, hc].bitcast(FP8X4), rhs_scale=grp["vs"][:, hc],
                                     start=True, stop=True)
             heads[i]["o_ps"] = o_ps
 
-        def dve_out(i, half):
+        def dve_recip(i):
+            recip = small.tile([P, NT], F32, tag="recip")
+            nc.vector.reciprocal(out=recip[:], in_=heads[i]["rsum"][:])
+            heads[i]["recip"] = recip
+
+        def dve_out(i):
             m, b, hh = where(i)
             grp = groups[m]
             hc = slice(hh * HD, (hh + 1) * HD)
-            if half == 0:
-                if hh == 0:
-                    o_sb = work.tile([P, NT, GC], F32, tag="o_sb", bufs=2)
-                    grp["o"] = o_sb
-                recip = small.tile([P, NT], F32, tag="recip")
-                nc.vector.reciprocal(out=recip[:], in_=heads[i]["rsum"][:])
-                heads[i]["recip"] = recip
-            th = slice(2 * half, 2 * half + 2)
-            nc.vector.tensor_tensor(out=grp["o"][:, th, hc], in0=heads[i]["o_ps"][:, th, :],
-                                    in1=heads[i]["recip"][:, th].unsqueeze(2).to_broadcast([P, 2, HD]), op=ALU.mult)
-            if half == 1 and hh == GH - 1:
+            if hh == 0:
+                o_sb = work.tile([P, NT, GC], F32, tag="o_sb", bufs=2)
+                grp["o"] = o_sb
+            nc.vector.tensor_tensor(out=grp["o"][:, :, hc], in0=heads[i]["o_ps"][:],
+                                    in1=heads[i]["recip"][:].unsqueeze(2).to_broadcast([P, NT, HD]), op=ALU.mult)
+            if hh == GH - 1:
                 g = m % NG
                 nc.sync.dma_start(out=o_dram[b, :, :, g * GC:(g + 1) * GC], in_=grp["o"][:])
 
@@ -236,8 +236,10 @@ def tile_knnattention_kernel(tc, model_hidden_states, k_hidden_states, k_embeddi
         setup_maskc(0)
         setup_mb_pe(0)
         setup_mb_copy(0)
+        for hh in range(GH):
+            pool_v_regroup(0, hh)
 
-        for s in range(TILES + LEAD + 15):
+        for s in range(TILES + LEAD + 13):
             x = s - LEAD
             if 0 <= x - 3 < TILES:
                 pe_e_transposes(x - 3)
@@ -250,24 +252,24 @@ def tile_knnattention_kernel(tc, model_hidden_states, k_hidden_states, k_embeddi
                 pe_pv((x - 11) // NT)
             if 0 <= x - 1 < TILES:
                 dve_max(x - 1)
-            if x >= 5 and (x - 5) % 2 == 0 and (x - 5) // 2 < TILES // 2:
-                dve_e_copy((x - 5) // 2)
-            if x >= 8 and (x - 8) % 2 == 0 and (x - 8) // 2 < TILES // 2:
-                dve_quant((x - 8) // 2)
+            if x >= 10 and (x - 10) % NT == 0 and (x - 10) // NT < HEADS:
+                dve_quant((x - 10) // NT)
+            if x >= 9 and (x - 9) % NT == 0 and (x - 9) // NT < HEADS:
+                dve_recip((x - 9) // NT)
             if x >= 12 and (x - 12) % NT == 0 and (x - 12) // NT < HEADS:
-                dve_out((x - 12) // NT, 0)
-            if x >= 14 and (x - 14) % NT == 0 and (x - 14) // NT < HEADS:
-                dve_out((x - 14) // NT, 1)
-            if x >= 5 and (x - 5) % NT == 0 and (x - 5) // NT < HEADS:
-                dve_v_quant((x - 5) // NT)
+                dve_out((x - 12) // NT)
+            if s >= 7 and (s - 7) % (GH * NT) == 0 and (s - 7) // (GH * NT) < B * NG:
+                dve_v_quant((s - 7) // (GH * NT))
             if 0 <= x - 2 < TILES:
                 act_exp(x - 2)
+            if x >= 5 and (x - 5) % 2 == 0 and (x - 5) // 2 < TILES // 2:
+                act_e_copy((x - 5) // 2)
             if i < HEADS and r == 3:
                 act_qk_copy(i)
             if x >= 6 and (x - 6) % 2 == 0 and (x - 6) // 2 < TILES // 2:
                 pool_regroup((x - 6) // 2)
-            if x >= 1 and (x - 1) % NT == 0 and (x - 1) // NT < HEADS:
-                pool_v_regroup((x - 1) // NT)
+            if s >= 9 and (s - 9) % NT == 0 and (s - 9) // NT + GH < HEADS:
+                pool_v_regroup((s - 9) // NT // GH + 1, (s - 9) // NT % GH)
             if s >= 22 and (s - 22) % (GH * NT) == 0 and (s - 22) // (GH * NT) + 3 < B * NG:
                 load_group((s - 22) // (GH * NT) + 3)
             for b in range(1, B):

@@ -29,8 +29,8 @@ def tile_knnattention_kernel(tc, model_hidden_states, k_hidden_states, k_embeddi
     nc = tc.nc
     scale = 1.0 / math.sqrt(HD)
     q_dram = model_hidden_states.rearrange("b (p t) c -> b p t c", t=NT)
-    k_dram = k_hidden_states.rearrange("b (p t) c -> b p t c", t=NT)
-    v_dram = k_embeddings.rearrange("b (p t) c -> b p t c", t=NT)
+    k_dram = k_hidden_states.rearrange("b (t p) c -> b p t c", t=NT)
+    v_dram = k_embeddings.rearrange("b (u p e) c -> b u p e c", u=2, e=2)
     o_dram = out.rearrange("b (p t) c -> b p t c", t=NT)
     with ExitStack() as ctx:
         const = ctx.enter_context(tc.tile_pool(name="const", bufs=1))
@@ -59,11 +59,12 @@ def tile_knnattention_kernel(tc, model_hidden_states, k_hidden_states, k_embeddi
             k_sb = loads.tile([P, NT, GC], BF16, tag="k")
             nc.sync.dma_start(out=k_sb[:], in_=k_dram[b, :, :, cols])
             v_sb = loads.tile([P, NT, GC], BF16, tag="v")
-            nc.sync.dma_start(out=v_sb[:], in_=v_dram[b, :, :, cols])
+            for u in range(2):
+                nc.sync.dma_start(out=v_sb[:, 2 * u:2 * u + 2, :], in_=v_dram[b, u, :, :, cols])
             groups[m] = {"q": q_sb, "k": k_sb, "v": v_sb}
 
         def setup_keep(b):
-            mask_k = batch[b]["mask"][:].rearrange("x (p j) -> x j p", j=NT)
+            mask_k = batch[b]["mask"][:].rearrange("x (j p) -> x j p", j=NT)
             keep = const.tile([P, NT, P], BF16, name="keep%d" % b)
             nc.vector.tensor_scalar(out=keep[:], in0=mask_k, scalar1=0.0, scalar2=None, op0=ALU.is_equal)
             diagk = const.tile([P, NT, P], BF16, name="diagk%d" % b)
@@ -72,7 +73,7 @@ def tile_knnattention_kernel(tc, model_hidden_states, k_hidden_states, k_embeddi
             batch[b]["diagk"] = diagk
 
         def setup_maskc(b):
-            mask_k = batch[b]["mask"][:].rearrange("x (p j) -> x j p", j=NT)
+            mask_k = batch[b]["mask"][:].rearrange("x (j p) -> x j p", j=NT)
             maskc = const.tile([P, NT, P], F32, name="maskc%d" % b)
             nc.vector.tensor_scalar(out=maskc[:], in0=mask_k, scalar1=math.sqrt(HD), scalar2=None, op0=ALU.mult)
             batch[b]["maskc"] = maskc
@@ -148,30 +149,26 @@ def tile_knnattention_kernel(tc, model_hidden_states, k_hidden_states, k_embeddi
         def pe_e_transposes(n):
             mp, tt = divmod(n, 2)
             if tt == 0:
-                et_ps = psum.tile([P, 2, NT, P], BF16, tag="et", bufs=3)
+                et_ps = psum.tile([P, 2, 2, P], F32, tag="et", bufs=3)
                 pairs[mp] = {"et_ps": et_ps}
-            for j in range(NT):
-                nc.tensor.transpose(pairs[mp]["et_ps"][:, tt, j, :], tiles[n]["e"][:, j * P:(j + 1) * P], ident_bf[:])
+            e_words = tiles[n]["e"][:].bitcast(F32)
+            for u in range(2):
+                nc.tensor.transpose(pairs[mp]["et_ps"][:, tt, u, :], e_words[:, u * P:(u + 1) * P], ident_f[:])
 
         def act_e_copy(mp):
-            et_sb = work.tile([P, 2, NT, P], BF16, tag="et_sb", bufs=3)
-            nc.scalar.copy(out=et_sb[:], in_=pairs[mp]["et_ps"][:])
-            pairs[mp]["et_sb"] = et_sb
-
-        def pool_regroup(mp):
             i, half = divmod(mp, 2)
             if half == 0:
-                eg = work.tile([P, NT, P, NT], BF16, tag="eg", bufs=3, align_bytes=64)
+                eg = work.tile([P, NT * P * NT], BF16, tag="eg", bufs=3, align_bytes=64)
                 heads[i]["eg"] = eg
-            nc.gpsimd.tensor_scalar(out=heads[i]["eg"][:, 2 * half:2 * half + 2, :, :],
-                                    in0=pairs[mp]["et_sb"][:].rearrange("p t j q -> p t q j"),
-                                    scalar1=1.0, scalar2=0.0, op0=ALU.mult, op1=ALU.add)
+            eg_words = heads[i]["eg"][:].bitcast(F32).rearrange("p (t q u) -> p t q u", t=NT, q=P, u=2)
+            nc.scalar.copy(out=eg_words[:, 2 * half:2 * half + 2, :, :],
+                           in_=pairs[mp]["et_ps"][:].rearrange("p t u q -> p t q u"))
 
         def dve_quant(i):
             e_codes = work.tile([P, S], U32, tag="ec", bufs=3, align_bytes=64)
             e_scales = work.tile([P, S], U8, tag="es", bufs=3, align_bytes=64)
             nc.vector.quantize_mx(out=e_codes[:].bitcast(FP8X4), scales=e_scales[:],
-                                  in_=heads[i]["eg"][:].rearrange("p t q j -> p (t q j)"))
+                                  in_=heads[i]["eg"][:])
             heads[i]["ec"] = e_codes
             heads[i]["es"] = e_scales
 
@@ -218,8 +215,10 @@ def tile_knnattention_kernel(tc, model_hidden_states, k_hidden_states, k_embeddi
                 grp["o"] = o_sb
             nc.vector.tensor_tensor(out=grp["o"][:, :, hc], in0=heads[i]["o_ps"][:],
                                     in1=heads[i]["recip"][:].unsqueeze(2).to_broadcast([P, NT, HD]), op=ALU.mult)
-            if hh == GH - 1:
-                g = m % NG
+            g = m % NG
+            if m == B * NG - 1:
+                nc.sync.dma_start(out=o_dram[b, :, :, g * GC + hh * HD:g * GC + (hh + 1) * HD], in_=grp["o"][:, :, hc])
+            elif hh == GH - 1:
                 nc.sync.dma_start(out=o_dram[b, :, :, g * GC:(g + 1) * GC], in_=grp["o"][:])
 
         load_mask(0)
@@ -248,26 +247,24 @@ def tile_knnattention_kernel(tc, model_hidden_states, k_hidden_states, k_embeddi
             i, r = divmod(s, NT)
             if i < HEADS and r < 3:
                 pe_qk_transposes(i, r)
-            if x >= 11 and (x - 11) % NT == 0 and (x - 11) // NT < HEADS:
-                pe_pv((x - 11) // NT)
+            if x >= 10 and (x - 10) % NT == 0 and (x - 10) // NT < HEADS:
+                pe_pv((x - 10) // NT)
             if 0 <= x - 1 < TILES:
                 dve_max(x - 1)
-            if x >= 10 and (x - 10) % NT == 0 and (x - 10) // NT < HEADS:
-                dve_quant((x - 10) // NT)
             if x >= 9 and (x - 9) % NT == 0 and (x - 9) // NT < HEADS:
-                dve_recip((x - 9) // NT)
-            if x >= 12 and (x - 12) % NT == 0 and (x - 12) // NT < HEADS:
-                dve_out((x - 12) // NT)
-            if s >= 7 and (s - 7) % (GH * NT) == 0 and (s - 7) // (GH * NT) < B * NG:
-                dve_v_quant((s - 7) // (GH * NT))
+                dve_quant((x - 9) // NT)
+            if x >= 8 and (x - 8) % NT == 0 and (x - 8) // NT < HEADS:
+                dve_recip((x - 8) // NT)
+            if x >= 11 and (x - 11) % NT == 0 and (x - 11) // NT < HEADS:
+                dve_out((x - 11) // NT)
+            if s >= 6 and (s - 6) % (GH * NT) == 0 and (s - 6) // (GH * NT) < B * NG:
+                dve_v_quant((s - 6) // (GH * NT))
             if 0 <= x - 2 < TILES:
                 act_exp(x - 2)
             if x >= 5 and (x - 5) % 2 == 0 and (x - 5) // 2 < TILES // 2:
                 act_e_copy((x - 5) // 2)
             if i < HEADS and r == 3:
                 act_qk_copy(i)
-            if x >= 6 and (x - 6) % 2 == 0 and (x - 6) // 2 < TILES // 2:
-                pool_regroup((x - 6) // 2)
             if s >= 9 and (s - 9) % NT == 0 and (s - 9) // NT + GH < HEADS:
                 pool_v_regroup((s - 9) // NT // GH + 1, (s - 9) // NT % GH)
             if s >= 22 and (s - 22) % (GH * NT) == 0 and (s - 22) // (GH * NT) + 3 < B * NG:

@@ -21,8 +21,6 @@ GH = 4
 NG = NH // GH
 GC = GH * HD
 HEADS = B * NH
-TILES = HEADS * NT
-LEAD = 6
 
 
 def tile_knnattention_kernel(tc, model_hidden_states, k_hidden_states, k_embeddings, attention_mask, out):
@@ -43,8 +41,6 @@ def tile_knnattention_kernel(tc, model_hidden_states, k_hidden_states, k_embeddi
         groups = {}
         batch = {}
         heads = {}
-        pairs = {}
-        tiles = {}
 
         def load_mask(b):
             mask_bf = const.tile([P, S], BF16, name="mask%d" % b)
@@ -79,7 +75,7 @@ def tile_knnattention_kernel(tc, model_hidden_states, k_hidden_states, k_embeddi
             batch[b]["maskc"] = maskc
 
         def setup_mb_pe(b):
-            mb_ps = psum.tile([P, NT, P], F32, tag="s", bufs=3)
+            mb_ps = psum.tile([P, NT, P], F32, tag="qk", bufs=1)
             for j in range(NT):
                 nc.tensor.transpose(mb_ps[:, j, :], batch[b]["maskc"][:, j, :], ident_f[:])
             batch[b]["mb_ps"] = mb_ps
@@ -93,82 +89,84 @@ def tile_knnattention_kernel(tc, model_hidden_states, k_hidden_states, k_embeddi
             m, hh = divmod(i, GH)
             return m, m // NG, hh
 
-        def pe_qk_transposes(i, part):
+        def pe_qk_transposes(i):
             m, b, hh = where(i)
             grp = groups[m]
             hc = slice(hh * HD, (hh + 1) * HD)
-            if part == 0:
-                qk_ps = psum.tile([P, 2 * S], BF16, tag="qk", bufs=1)
-                heads[i] = {"qk_ps": qk_ps}
-            qk_ps = heads[i]["qk_ps"]
-            for x in ((0, 1, 2), (3, 4, 5), (6, 7))[part]:
-                if x < NT:
-                    nc.tensor.transpose(qk_ps[:, x * P:(x + 1) * P], grp["q"][:, x, hc], ident_bf[:])
-                else:
-                    nc.tensor.transpose(qk_ps[:, x * P:(x + 1) * P], grp["k"][:, x - NT, hc],
-                                        batch[b]["diagk"][:, x - NT, :])
+            qk_ps = psum.tile([P, 2 * S], BF16, tag="qk", bufs=1)
+            for t in range(NT):
+                nc.tensor.transpose(qk_ps[:, t * P:(t + 1) * P], grp["q"][:, t, hc], ident_bf[:])
+            for j in range(NT):
+                nc.tensor.transpose(qk_ps[:, S + j * P:S + (j + 1) * P], grp["k"][:, j, hc], batch[b]["diagk"][:, j, :])
+            heads[i] = {"qk_ps": qk_ps}
 
         def act_qk_copy(i):
             qkt = work.tile([P, 2 * S], BF16, tag="qkt", bufs=3)
             nc.scalar.copy(out=qkt[:], in_=heads[i]["qk_ps"][:])
             heads[i]["qkt"] = qkt
 
-        def pe_scores(n):
-            i, t = divmod(n, NT)
+        def pe_deposit(i):
             m, b, hh = where(i)
-            qkt = heads[i]["qkt"]
             mb = batch[b]["mb"]
-            s_ps = psum.tile([P, S], F32, tag="s", bufs=3)
-            for j in range(NT):
-                nc.tensor.matmul(out=s_ps[:, j * P:(j + 1) * P], lhsT=mb[:, j, :], rhs=ident_f[:],
-                                 is_transpose=True, start=(j == 0), stop=False)
-            nc.tensor.matmul(out=s_ps[:], lhsT=qkt[:, t * P:(t + 1) * P], rhs=qkt[:, S:2 * S],
-                             start=False, stop=True)
-            tiles[n] = {"s": s_ps}
+            banks = []
+            for t in range(NT):
+                s_ps = psum.tile([P, S], F32, tag="s", bufs=4)
+                for j in range(NT):
+                    nc.tensor.matmul(out=s_ps[:, j * P:(j + 1) * P], lhsT=mb[:, j, :], rhs=ident_f[:],
+                                     is_transpose=True, start=(j == 0), stop=False)
+                banks.append(s_ps)
+            heads[i]["s"] = banks
 
-        def dve_max(n):
-            i, t = divmod(n, NT)
-            if t == 0:
-                bias = small.tile([P, NT], F32, tag="bias")
-                heads[i]["bias"] = bias
-            y_sb = work.tile([P, S], F32, tag="y", bufs=4)
-            nc.vector.tensor_scalar(out=y_sb[:], in0=tiles[n]["s"][:], scalar1=-scale, scalar2=None, op0=ALU.mult,
-                                    op1=ALU.min, accum_out=heads[i]["bias"][:, t:t + 1])
-            tiles[n]["y"] = y_sb
+        def pe_scores(i):
+            qkt = heads[i]["qkt"]
+            for t in range(NT):
+                nc.tensor.matmul(out=heads[i]["s"][t][:], lhsT=qkt[:, t * P:(t + 1) * P], rhs=qkt[:, S:2 * S],
+                                 start=False, stop=True)
 
-        def act_exp(n):
-            i, t = divmod(n, NT)
+        def dve_max(i):
+            bias = small.tile([P, NT], F32, tag="bias")
+            ys = []
+            for t in range(NT):
+                y_sb = work.tile([P, S], F32, tag="y", bufs=6)
+                nc.vector.tensor_scalar(out=y_sb[:], in0=heads[i]["s"][t][:], scalar1=-scale, scalar2=None,
+                                        op0=ALU.mult, op1=ALU.min, accum_out=bias[:, t:t + 1])
+                ys.append(y_sb)
+            heads[i]["bias"] = bias
+            heads[i]["y"] = ys
+
+        def act_exp(i, t):
             if t == 0:
                 rsum = small.tile([P, NT], F32, tag="rsum")
                 heads[i]["rsum"] = rsum
-            e_sb = work.tile([P, S], BF16, tag="e", bufs=4)
-            nc.scalar.activation(out=e_sb[:], in_=tiles[n]["y"][:], func=ACTF.Exp, bias=heads[i]["bias"][:, t:t + 1],
-                                 scale=-1.0, accum_out=heads[i]["rsum"][:, t:t + 1])
-            tiles[n]["e"] = e_sb
+                e_sb = work.tile([P, NT, S], BF16, tag="e", bufs=4)
+                heads[i]["e"] = e_sb
+            nc.scalar.activation(out=heads[i]["e"][:, t, :], in_=heads[i]["y"][t][:], func=ACTF.Exp,
+                                 bias=heads[i]["bias"][:, t:t + 1], scale=-1.0,
+                                 accum_out=heads[i]["rsum"][:, t:t + 1])
 
-        def pe_e_transposes(n):
-            mp, tt = divmod(n, 2)
-            if tt == 0:
-                et_ps = psum.tile([P, 2, 2, P], F32, tag="et", bufs=3)
-                pairs[mp] = {"et_ps": et_ps}
-            e_words = tiles[n]["e"][:].bitcast(F32)
-            for u in range(2):
-                nc.tensor.transpose(pairs[mp]["et_ps"][:, tt, u, :], e_words[:, u * P:(u + 1) * P], ident_f[:])
+        def pe_e_transposes(i):
+            banks = []
+            for half in range(2):
+                et_ps = psum.tile([P, 2, 2, P], F32, tag="et", bufs=2)
+                for tt in range(2):
+                    e_words = heads[i]["e"][:, 2 * half + tt, :].bitcast(F32)
+                    for u in range(2):
+                        nc.tensor.transpose(et_ps[:, tt, u, :], e_words[:, u * P:(u + 1) * P], ident_f[:])
+                banks.append(et_ps)
+            heads[i]["et"] = banks
 
-        def act_e_copy(mp):
-            i, half = divmod(mp, 2)
-            if half == 0:
-                eg = work.tile([P, NT * P * NT], BF16, tag="eg", bufs=3, align_bytes=64)
-                heads[i]["eg"] = eg
-            eg_words = heads[i]["eg"][:].bitcast(F32).rearrange("p (t q u) -> p t q u", t=NT, q=P, u=2)
-            nc.scalar.copy(out=eg_words[:, 2 * half:2 * half + 2, :, :],
-                           in_=pairs[mp]["et_ps"][:].rearrange("p t u q -> p t q u"))
+        def act_e_copy(i):
+            eg = work.tile([P, NT * P * NT], BF16, tag="eg", bufs=3, align_bytes=64)
+            eg_words = eg[:].bitcast(F32).rearrange("p (t q u) -> p t q u", t=NT, q=P, u=2)
+            for half in range(2):
+                nc.scalar.copy(out=eg_words[:, 2 * half:2 * half + 2, :, :],
+                               in_=heads[i]["et"][half][:].rearrange("p t u q -> p t q u"))
+            heads[i]["eg"] = eg
 
         def dve_quant(i):
             e_codes = work.tile([P, S], U32, tag="ec", bufs=3, align_bytes=64)
             e_scales = work.tile([P, S], U8, tag="es", bufs=3, align_bytes=64)
-            nc.vector.quantize_mx(out=e_codes[:].bitcast(FP8X4), scales=e_scales[:],
-                                  in_=heads[i]["eg"][:])
+            nc.vector.quantize_mx(out=e_codes[:].bitcast(FP8X4), scales=e_scales[:], in_=heads[i]["eg"][:])
             heads[i]["ec"] = e_codes
             heads[i]["es"] = e_scales
 
@@ -194,9 +192,9 @@ def tile_knnattention_kernel(tc, model_hidden_states, k_hidden_states, k_embeddi
             hc = slice(hh * HD, (hh + 1) * HD)
             o_ps = psum.tile([P, NT, HD], F32, tag="o", bufs=1)
             for t in range(NT):
-                pr = heads[i]
                 tq = slice(t * P, (t + 1) * P)
-                nc.tensor.matmul_mx(out=o_ps[:, t, :], lhsT=pr["ec"][:, tq].bitcast(FP8X4), lhsT_scale=pr["es"][:, tq],
+                nc.tensor.matmul_mx(out=o_ps[:, t, :], lhsT=heads[i]["ec"][:, tq].bitcast(FP8X4),
+                                    lhsT_scale=heads[i]["es"][:, tq],
                                     rhs=grp["vc"][:, hc].bitcast(FP8X4), rhs_scale=grp["vs"][:, hc],
                                     start=True, stop=True)
             heads[i]["o_ps"] = o_ps
@@ -237,45 +235,48 @@ def tile_knnattention_kernel(tc, model_hidden_states, k_hidden_states, k_embeddi
         setup_mb_copy(0)
         for hh in range(GH):
             pool_v_regroup(0, hh)
+        pe_qk_transposes(0)
+        act_qk_copy(0)
 
-        for s in range(TILES + LEAD + 13):
-            x = s - LEAD
-            if 0 <= x - 3 < TILES:
-                pe_e_transposes(x - 3)
-            if 0 <= x < TILES:
-                pe_scores(x)
-            i, r = divmod(s, NT)
-            if i < HEADS and r < 3:
-                pe_qk_transposes(i, r)
-            if x >= 10 and (x - 10) % NT == 0 and (x - 10) // NT < HEADS:
-                pe_pv((x - 10) // NT)
-            if 0 <= x - 1 < TILES:
-                dve_max(x - 1)
-            if x >= 9 and (x - 9) % NT == 0 and (x - 9) // NT < HEADS:
-                dve_quant((x - 9) // NT)
-            if x >= 8 and (x - 8) % NT == 0 and (x - 8) // NT < HEADS:
-                dve_recip((x - 8) // NT)
-            if x >= 11 and (x - 11) % NT == 0 and (x - 11) // NT < HEADS:
-                dve_out((x - 11) // NT)
-            if s >= 6 and (s - 6) % (GH * NT) == 0 and (s - 6) // (GH * NT) < B * NG:
-                dve_v_quant((s - 6) // (GH * NT))
-            if 0 <= x - 2 < TILES:
-                act_exp(x - 2)
-            if x >= 5 and (x - 5) % 2 == 0 and (x - 5) // 2 < TILES // 2:
-                act_e_copy((x - 5) // 2)
-            if i < HEADS and r == 3:
-                act_qk_copy(i)
-            if s >= 9 and (s - 9) % NT == 0 and (s - 9) // NT + GH < HEADS:
-                pool_v_regroup((s - 9) // NT // GH + 1, (s - 9) // NT % GH)
-            if s >= 22 and (s - 22) % (GH * NT) == 0 and (s - 22) // (GH * NT) + 3 < B * NG:
-                load_group((s - 22) // (GH * NT) + 3)
+        for h in range(HEADS + 3):
+            live = h < HEADS
+            if 0 <= h - 2 < HEADS:
+                pe_e_transposes(h - 2)
+            if live:
+                pe_deposit(h)
+                pe_scores(h)
+            if h + 1 < HEADS:
+                pe_qk_transposes(h + 1)
+            if 0 <= h - 3:
+                pe_pv(h - 3)
+            if 0 <= h - 2 < HEADS:
+                act_e_copy(h - 2)
+            if live:
+                dve_max(h)
+                act_exp(h, 0)
+            if h + 1 < HEADS:
+                act_qk_copy(h + 1)
             for b in range(1, B):
-                base = NH * NT * (b - 1) + LEAD + 20
-                if s == base:
-                    setup_keep(b)
-                if s == base + 1:
-                    setup_maskc(b)
-                if s == base + 2:
+                if h == NH * b - 5:
                     setup_mb_pe(b)
-                if s == base + 3:
+            if live:
+                for t in range(1, NT):
+                    act_exp(h, t)
+            if 0 <= h - 3:
+                dve_recip(h - 3)
+            if 0 <= h - 2 < HEADS:
+                dve_quant(h - 2)
+            if 0 <= h - 3:
+                dve_out(h - 3)
+            if h % GH == 0 and h // GH < B * NG:
+                dve_v_quant(h // GH)
+            for b in range(1, B):
+                if h == NH * b - 6:
+                    setup_keep(b)
+                    setup_maskc(b)
+                if h == NH * b - 5:
                     setup_mb_copy(b)
+            if h + GH < HEADS:
+                pool_v_regroup(h // GH + 1, h % GH)
+            if h % GH == 3 and h // GH + 3 < B * NG:
+                load_group(h // GH + 3)

@@ -89,16 +89,20 @@ def tile_knnattention_kernel(tc, model_hidden_states, k_hidden_states, k_embeddi
             m, hh = divmod(i, GH)
             return m, m // NG, hh
 
-        def pe_qk_transposes(i):
+        def pe_qk_transposes(i, part):
             m, b, hh = where(i)
             grp = groups[m]
             hc = slice(hh * HD, (hh + 1) * HD)
-            qk_ps = psum.tile([P, 2 * S], BF16, tag="qk", bufs=1)
-            for t in range(NT):
-                nc.tensor.transpose(qk_ps[:, t * P:(t + 1) * P], grp["q"][:, t, hc], ident_bf[:])
-            for j in range(NT):
-                nc.tensor.transpose(qk_ps[:, S + j * P:S + (j + 1) * P], grp["k"][:, j, hc], batch[b]["diagk"][:, j, :])
-            heads[i] = {"qk_ps": qk_ps}
+            if part == 0:
+                qk_ps = psum.tile([P, 2 * S], BF16, tag="qk", bufs=1)
+                heads[i] = {"qk_ps": qk_ps}
+            qk_ps = heads[i]["qk_ps"]
+            for x in (2 * part, 2 * part + 1):
+                if x < NT:
+                    nc.tensor.transpose(qk_ps[:, x * P:(x + 1) * P], grp["q"][:, x, hc], ident_bf[:])
+                else:
+                    nc.tensor.transpose(qk_ps[:, x * P:(x + 1) * P], grp["k"][:, x - NT, hc],
+                                        batch[b]["diagk"][:, x - NT, :])
 
         def act_qk_copy(i):
             qkt = work.tile([P, 2 * S], BF16, tag="qkt", bufs=3)
@@ -117,11 +121,10 @@ def tile_knnattention_kernel(tc, model_hidden_states, k_hidden_states, k_embeddi
                 banks.append(s_ps)
             heads[i]["s"] = banks
 
-        def pe_scores(i):
+        def pe_scores(i, t):
             qkt = heads[i]["qkt"]
-            for t in range(NT):
-                nc.tensor.matmul(out=heads[i]["s"][t][:], lhsT=qkt[:, t * P:(t + 1) * P], rhs=qkt[:, S:2 * S],
-                                 start=False, stop=True)
+            nc.tensor.matmul(out=heads[i]["s"][t][:], lhsT=qkt[:, t * P:(t + 1) * P], rhs=qkt[:, S:2 * S],
+                             start=False, stop=True)
 
         def dve_max(i):
             bias = small.tile([P, NT], F32, tag="bias")
@@ -235,7 +238,8 @@ def tile_knnattention_kernel(tc, model_hidden_states, k_hidden_states, k_embeddi
         setup_mb_copy(0)
         for hh in range(GH):
             pool_v_regroup(0, hh)
-        pe_qk_transposes(0)
+        for t in range(NT):
+            pe_qk_transposes(0, t)
         act_qk_copy(0)
 
         for h in range(HEADS + 3):
@@ -244,9 +248,10 @@ def tile_knnattention_kernel(tc, model_hidden_states, k_hidden_states, k_embeddi
                 pe_e_transposes(h - 2)
             if live:
                 pe_deposit(h)
-                pe_scores(h)
-            if h + 1 < HEADS:
-                pe_qk_transposes(h + 1)
+                for t in range(NT):
+                    if h + 1 < HEADS:
+                        pe_qk_transposes(h + 1, t)
+                    pe_scores(h, t)
             if 0 <= h - 3:
                 pe_pv(h - 3)
             if 0 <= h - 2 < HEADS:

@@ -51,9 +51,14 @@ def tile_knnattention_kernel(tc, model_hidden_states, k_hidden_states, k_embeddi
             b, g = divmod(m, NG)
             cols = slice(g * GC, (g + 1) * GC)
             q_sb = loads.tile([P, NT, GC], BF16, tag="q")
-            nc.sync.dma_start(out=q_sb[:], in_=q_dram[b, :, :, cols])
             k_sb = loads.tile([P, NT, GC], BF16, tag="k")
-            nc.sync.dma_start(out=k_sb[:], in_=k_dram[b, :, :, cols])
+            pieces = 2 if m == 0 else 1
+            width = GC // pieces
+            for piece in range(pieces):
+                part = slice(piece * width, (piece + 1) * width)
+                src = slice(g * GC + piece * width, g * GC + (piece + 1) * width)
+                nc.sync.dma_start(out=q_sb[:, :, part], in_=q_dram[b, :, :, src])
+                nc.sync.dma_start(out=k_sb[:, :, part], in_=k_dram[b, :, :, src])
             v_sb = loads.tile([P, NT, GC], BF16, tag="v")
             for u in range(2):
                 nc.sync.dma_start(out=v_sb[:, 2 * u:2 * u + 2, :], in_=v_dram[b, u, :, :, cols])
@@ -104,22 +109,24 @@ def tile_knnattention_kernel(tc, model_hidden_states, k_hidden_states, k_embeddi
                     nc.tensor.transpose(qk_ps[:, x * P:(x + 1) * P], grp["k"][:, x - NT, hc],
                                         batch[b]["diagk"][:, x - NT, :])
 
-        def act_qk_copy(i):
+        def qk_copy(i):
             qkt = work.tile([P, 2 * S], BF16, tag="qkt", bufs=3)
-            nc.scalar.copy(out=qkt[:], in_=heads[i]["qk_ps"][:])
+            if i % 3 == 0 and i > 0:
+                nc.vector.tensor_copy(out=qkt[:], in_=heads[i]["qk_ps"][:])
+            else:
+                nc.scalar.copy(out=qkt[:], in_=heads[i]["qk_ps"][:])
             heads[i]["qkt"] = qkt
 
-        def pe_deposit(i):
+        def pe_deposit(i, t):
             m, b, hh = where(i)
             mb = batch[b]["mb"]
-            banks = []
-            for t in range(NT):
-                s_ps = psum.tile([P, S], F32, tag="s", bufs=4)
-                for j in range(NT):
-                    nc.tensor.matmul(out=s_ps[:, j * P:(j + 1) * P], lhsT=mb[:, j, :], rhs=ident_f[:],
-                                     is_transpose=True, start=(j == 0), stop=False)
-                banks.append(s_ps)
-            heads[i]["s"] = banks
+            if t == 0:
+                heads[i]["s"] = []
+            s_ps = psum.tile([P, S], F32, tag="s", bufs=4)
+            for j in range(NT):
+                nc.tensor.matmul(out=s_ps[:, j * P:(j + 1) * P], lhsT=mb[:, j, :], rhs=ident_f[:],
+                                 is_transpose=True, start=(j == 0), stop=False)
+            heads[i]["s"].append(s_ps)
 
         def pe_scores(i, t):
             qkt = heads[i]["qkt"]
@@ -214,12 +221,20 @@ def tile_knnattention_kernel(tc, model_hidden_states, k_hidden_states, k_embeddi
             if hh == 0:
                 o_sb = work.tile([P, NT, GC], F32, tag="o_sb", bufs=2)
                 grp["o"] = o_sb
-            nc.vector.tensor_tensor(out=grp["o"][:, :, hc], in0=heads[i]["o_ps"][:],
-                                    in1=heads[i]["recip"][:].unsqueeze(2).to_broadcast([P, NT, HD]), op=ALU.mult)
             g = m % NG
+            oc = slice(g * GC + hh * HD, g * GC + (hh + 1) * HD)
+            cuts = 2 if i == HEADS - 1 else 1
+            rows = NT // cuts
+            for cut in range(cuts):
+                th = slice(cut * rows, (cut + 1) * rows)
+                nc.vector.tensor_tensor(out=grp["o"][:, th, hc], in0=heads[i]["o_ps"][:, th, :],
+                                        in1=heads[i]["recip"][:, th].unsqueeze(2).to_broadcast([P, rows, HD]),
+                                        op=ALU.mult)
+                if m == B * NG - 1:
+                    nc.sync.dma_start(out=o_dram[b, :, th, oc], in_=grp["o"][:, th, hc])
             if m == B * NG - 1:
-                nc.sync.dma_start(out=o_dram[b, :, :, g * GC + hh * HD:g * GC + (hh + 1) * HD], in_=grp["o"][:, :, hc])
-            elif hh == GH - 1:
+                return
+            if hh == GH - 1:
                 nc.sync.dma_start(out=o_dram[b, :, :, g * GC:(g + 1) * GC], in_=grp["o"][:])
 
         load_mask(0)
@@ -232,23 +247,27 @@ def tile_knnattention_kernel(tc, model_hidden_states, k_hidden_states, k_embeddi
         make_identity(nc, ident_bf[:])
         ident_f = const.tile([P, P], F32)
         make_identity(nc, ident_f[:])
-        setup_keep(0)
         setup_maskc(0)
         setup_mb_pe(0)
+        setup_keep(0)
         setup_mb_copy(0)
         for hh in range(GH):
             pool_v_regroup(0, hh)
         for t in range(NT):
             pe_qk_transposes(0, t)
-        act_qk_copy(0)
+        qk_copy(0)
 
         for h in range(HEADS + 3):
             live = h < HEADS
             if 0 <= h - 2 < HEADS:
                 pe_e_transposes(h - 2)
             if live:
-                pe_deposit(h)
+                if h > 0:
+                    for t in range(NT):
+                        pe_deposit(h, t)
                 for t in range(NT):
+                    if h == 0:
+                        pe_deposit(h, t)
                     if h + 1 < HEADS:
                         pe_qk_transposes(h + 1, t)
                     pe_scores(h, t)
@@ -260,7 +279,7 @@ def tile_knnattention_kernel(tc, model_hidden_states, k_hidden_states, k_embeddi
                 dve_max(h)
                 act_exp(h, 0)
             if h + 1 < HEADS:
-                act_qk_copy(h + 1)
+                qk_copy(h + 1)
             for b in range(1, B):
                 if h == NH * b - 5:
                     setup_mb_pe(b)

import math
from contextlib import ExitStack

import concourse.mybir as mybir
from concourse.masks import make_identity

B, S, NH, HD = 4, 512, 12, 128
FLOPS = 2 * 2 * B * NH * S * S * HD

BF16 = mybir.dt.bfloat16
F32 = mybir.dt.float32
U32 = mybir.dt.uint32
U8 = mybir.dt.uint8
FP8X4 = mybir.dt.float8_e4m3fn_x4
ALU = mybir.AluOpType
ACTF = mybir.ActivationFunctionType

P = 128
NT = S // P
GH = 4
NG = NH // GH
GC = GH * HD
HEADS = B * NH


def tile_knnattention_kernel(tc, model_hidden_states, k_hidden_states, k_embeddings, attention_mask, out):
    nc = tc.nc
    scale = 1.0 / math.sqrt(HD)
    q_dram = model_hidden_states.rearrange("b (p t) c -> b p t c", t=NT)
    k_dram = k_hidden_states.rearrange("b (t p) c -> b p t c", t=NT)
    v_dram = k_embeddings.rearrange("b (u p e) c -> b u p e c", u=2, e=2)
    o_dram = out.rearrange("b (p t) c -> b p t c", t=NT)
    with ExitStack() as ctx:
        const = ctx.enter_context(tc.tile_pool(name="const", bufs=1))
        loads = ctx.enter_context(tc.tile_pool(name="loads", bufs=3))
        work = ctx.enter_context(tc.tile_pool(name="work", bufs=3))
        small = ctx.enter_context(tc.tile_pool(name="small", bufs=6))
        psum = ctx.enter_context(tc.psum_pool(name="psum", bufs=1))
        ctx.enter_context(tc.manual_schedule())

        groups = {}
        batch = {}
        heads = {}

        def load_mask(b):
            mask_bf = const.tile([P, S], BF16, name="mask%d" % b)
            nc.sync.dma_start(out=mask_bf[:], in_=attention_mask[b, :].partition_broadcast(P))
            batch[b] = {"mask": mask_bf}

        def load_group(m):
            b, g = divmod(m, NG)
            cols = slice(g * GC, (g + 1) * GC)
            q_sb = loads.tile([P, NT, GC], BF16, tag="q")
            k_sb = loads.tile([P, NT, GC], BF16, tag="k")
            pieces = 2 if m == 0 else 1
            width = GC // pieces
            for piece in range(pieces):
                part = slice(piece * width, (piece + 1) * width)
                src = slice(g * GC + piece * width, g * GC + (piece + 1) * width)
                nc.sync.dma_start(out=q_sb[:, :, part], in_=q_dram[b, :, :, src])
                nc.sync.dma_start(out=k_sb[:, :, part], in_=k_dram[b, :, :, src])
            v_sb = loads.tile([P, NT, GC], BF16, tag="v")
            for u in range(2):
                nc.sync.dma_start(out=v_sb[:, 2 * u:2 * u + 2, :], in_=v_dram[b, u, :, :, cols])
            groups[m] = {"q": q_sb, "k": k_sb, "v": v_sb}

        def setup_keep(b):
            mask_k = batch[b]["mask"][:].rearrange("x (j p) -> x j p", j=NT)
            keep = const.tile([P, NT, P], BF16, name="keep%d" % b)
            nc.vector.tensor_scalar(out=keep[:], in0=mask_k, scalar1=0.0, scalar2=None, op0=ALU.is_equal)
            diagk = const.tile([P, NT, P], BF16, name="diagk%d" % b)
            nc.vector.tensor_tensor(out=diagk[:], in0=keep[:],
                                    in1=ident_bf[:].unsqueeze(1).to_broadcast([P, NT, P]), op=ALU.mult)
            batch[b]["diagk"] = diagk

        def setup_maskc(b):
            mask_k = batch[b]["mask"][:].rearrange("x (j p) -> x j p", j=NT)
            maskc = const.tile([P, NT, P], F32, name="maskc%d" % b)
            nc.vector.tensor_scalar(out=maskc[:], in0=mask_k, scalar1=math.sqrt(HD), scalar2=None, op0=ALU.mult)
            batch[b]["maskc"] = maskc

        def setup_mb_pe(b):
            mb_ps = psum.tile([P, NT, P], F32, tag="qk", bufs=1)
            for j in range(NT):
                nc.tensor.transpose(mb_ps[:, j, :], batch[b]["maskc"][:, j, :], ident_f[:])
            batch[b]["mb_ps"] = mb_ps

        def setup_mb_copy(b):
            mb = const.tile([P, NT, P], F32, name="mb%d" % b)
            nc.vector.tensor_copy(out=mb[:], in_=batch[b]["mb_ps"][:])
            batch[b]["mb"] = mb

        def where(i):
            m, hh = divmod(i, GH)
            return m, m // NG, hh

        def pe_qk_transposes(i, part):
            m, b, hh = where(i)
            grp = groups[m]
            hc = slice(hh * HD, (hh + 1) * HD)
            if part == 0:
                qk_ps = psum.tile([P, 2 * S], BF16, tag="qk", bufs=1)
                heads[i] = {"qk_ps": qk_ps}
            qk_ps = heads[i]["qk_ps"]
            for x in (2 * part, 2 * part + 1):
                if x < NT:
                    nc.tensor.transpose(qk_ps[:, x * P:(x + 1) * P], grp["q"][:, x, hc], ident_bf[:])
                else:
                    nc.tensor.transpose(qk_ps[:, x * P:(x + 1) * P], grp["k"][:, x - NT, hc],
                                        batch[b]["diagk"][:, x - NT, :])

        def qk_copy(i):
            qkt = work.tile([P, 2 * S], BF16, tag="qkt", bufs=3)
            if i % 3 == 0 and i > 0:
                nc.vector.tensor_copy(out=qkt[:], in_=heads[i]["qk_ps"][:])
            else:
                nc.scalar.copy(out=qkt[:], in_=heads[i]["qk_ps"][:])
            heads[i]["qkt"] = qkt

        def pe_deposit(i, t):
            m, b, hh = where(i)
            mb = batch[b]["mb"]
            if t == 0:
                heads[i]["s"] = []
            s_ps = psum.tile([P, S], F32, tag="s", bufs=4)
            for j in range(NT):
                nc.tensor.matmul(out=s_ps[:, j * P:(j + 1) * P], lhsT=mb[:, j, :], rhs=ident_f[:],
                                 is_transpose=True, start=(j == 0), stop=False)
            heads[i]["s"].append(s_ps)

        def pe_scores(i, t):
            qkt = heads[i]["qkt"]
            nc.tensor.matmul(out=heads[i]["s"][t][:], lhsT=qkt[:, t * P:(t + 1) * P], rhs=qkt[:, S:2 * S],
                             start=False, stop=True)

        def dve_max(i):
            bias = small.tile([P, NT], F32, tag="bias")
            ys = []
            for t in range(NT):
                y_sb = work.tile([P, S], F32, tag="y", bufs=6)
                nc.vector.tensor_scalar(out=y_sb[:], in0=heads[i]["s"][t][:], scalar1=-scale, scalar2=None,
                                        op0=ALU.mult, op1=ALU.min, accum_out=bias[:, t:t + 1])
                ys.append(y_sb)
            heads[i]["bias"] = bias
            heads[i]["y"] = ys

        def act_exp(i, t):
            if t == 0:
                rsum = small.tile([P, NT], F32, tag="rsum")
                heads[i]["rsum"] = rsum
                e_sb = work.tile([P, NT, S], BF16, tag="e", bufs=4)
                heads[i]["e"] = e_sb
            nc.scalar.activation(out=heads[i]["e"][:, t, :], in_=heads[i]["y"][t][:], func=ACTF.Exp,
                                 bias=heads[i]["bias"][:, t:t + 1], scale=-1.0,
                                 accum_out=heads[i]["rsum"][:, t:t + 1])

        def pe_e_transposes(i):
            banks = []
            for half in range(2):
                et_ps = psum.tile([P, 2, 2, P], F32, tag="et", bufs=2)
                for tt in range(2):
                    e_words = heads[i]["e"][:, 2 * half + tt, :].bitcast(F32)
                    for u in range(2):
                        nc.tensor.transpose(et_ps[:, tt, u, :], e_words[:, u * P:(u + 1) * P], ident_f[:])
                banks.append(et_ps)
            heads[i]["et"] = banks

        def act_e_copy(i):
            eg = work.tile([P, NT * P * NT], BF16, tag="eg", bufs=3, align_bytes=64)
            eg_words = eg[:].bitcast(F32).rearrange("p (t q u) -> p t q u", t=NT, q=P, u=2)
            for half in range(2):
                nc.scalar.copy(out=eg_words[:, 2 * half:2 * half + 2, :, :],
                               in_=heads[i]["et"][half][:].rearrange("p t u q -> p t q u"))
            heads[i]["eg"] = eg

        def dve_quant(i):
            e_codes = work.tile([P, S], U32, tag="ec", bufs=3, align_bytes=64)
            e_scales = work.tile([P, S], U8, tag="es", bufs=3, align_bytes=64)
            nc.vector.quantize_mx(out=e_codes[:].bitcast(FP8X4), scales=e_scales[:], in_=heads[i]["eg"][:])
            heads[i]["ec"] = e_codes
            heads[i]["es"] = e_scales

        def pool_v_regroup(m, hh):
            hc = slice(hh * HD, (hh + 1) * HD)
            if hh == 0:
                vg = work.tile([P, GC, NT], BF16, tag="vg", bufs=2, align_bytes=64)
                groups[m]["vg"] = vg
            nc.gpsimd.tensor_scalar(out=groups[m]["vg"][:, hc, :], in0=groups[m]["v"][:, :, hc].rearrange("p j c -> p c j"),
                                    scalar1=1.0, scalar2=0.0, op0=ALU.mult, op1=ALU.add)

        def dve_v_quant(m):
            v_codes = work.tile([P, GC], U32, tag="vc", bufs=3, align_bytes=64)
            v_scales = work.tile([P, GC], U8, tag="vs", bufs=3, align_bytes=64)
            nc.vector.quantize_mx(out=v_codes[:].bitcast(FP8X4), scales=v_scales[:],
                                  in_=groups[m]["vg"][:].rearrange("p c j -> p (c j)"))
            groups[m]["vc"] = v_codes
            groups[m]["vs"] = v_scales

        def pe_pv(i):
            m, b, hh = where(i)
            grp = groups[m]
            hc = slice(hh * HD, (hh + 1) * HD)
            o_ps = psum.tile([P, NT, HD], F32, tag="o", bufs=1)
            for t in range(NT):
                tq = slice(t * P, (t + 1) * P)
                nc.tensor.matmul_mx(out=o_ps[:, t, :], lhsT=heads[i]["ec"][:, tq].bitcast(FP8X4),
                                    lhsT_scale=heads[i]["es"][:, tq],
                                    rhs=grp["vc"][:, hc].bitcast(FP8X4), rhs_scale=grp["vs"][:, hc],
                                    start=True, stop=True)
            heads[i]["o_ps"] = o_ps

        def dve_recip(i):
            recip = small.tile([P, NT], F32, tag="recip")
            nc.vector.reciprocal(out=recip[:], in_=heads[i]["rsum"][:])
            heads[i]["recip"] = recip

        def dve_out(i):
            m, b, hh = where(i)
            grp = groups[m]
            hc = slice(hh * HD, (hh + 1) * HD)
            if hh == 0:
                o_sb = work.tile([P, NT, GC], F32, tag="o_sb", bufs=2)
                grp["o"] = o_sb
            g = m % NG
            oc = slice(g * GC + hh * HD, g * GC + (hh + 1) * HD)
            cuts = 2 if i == HEADS - 1 else 1
            rows = NT // cuts
            for cut in range(cuts):
                th = slice(cut * rows, (cut + 1) * rows)
                nc.vector.tensor_tensor(out=grp["o"][:, th, hc], in0=heads[i]["o_ps"][:, th, :],
                                        in1=heads[i]["recip"][:, th].unsqueeze(2).to_broadcast([P, rows, HD]),
                                        op=ALU.mult)
                if m == B * NG - 1:
                    nc.sync.dma_start(out=o_dram[b, :, th, oc], in_=grp["o"][:, th, hc])
            if m == B * NG - 1:
                return
            if hh == GH - 1:
                nc.sync.dma_start(out=o_dram[b, :, :, g * GC:(g + 1) * GC], in_=grp["o"][:])

        load_mask(0)
        load_group(0)
        for b in range(1, B):
            load_mask(b)
        load_group(1)
        load_group(2)
        ident_bf = const.tile([P, P], BF16)
        make_identity(nc, ident_bf[:])
        ident_f = const.tile([P, P], F32)
        make_identity(nc, ident_f[:])
        setup_maskc(0)
        setup_mb_pe(0)
        setup_keep(0)
        setup_mb_copy(0)
        for hh in range(GH):
            pool_v_regroup(0, hh)
        for t in range(NT):
            pe_qk_transposes(0, t)
        qk_copy(0)

        for h in range(HEADS + 3):
            live = h < HEADS
            if 0 <= h - 2 < HEADS:
                pe_e_transposes(h - 2)
            if live:
                if h > 0:
                    for t in range(NT):
                        pe_deposit(h, t)
                for t in range(NT):
                    if h == 0:
                        pe_deposit(h, t)
                    if h + 1 < HEADS:
                        pe_qk_transposes(h + 1, t)
                    pe_scores(h, t)
            if 0 <= h - 3:
                pe_pv(h - 3)
            if 0 <= h - 2 < HEADS:
                act_e_copy(h - 2)
            if live:
                dve_max(h)
                act_exp(h, 0)
            if h + 1 < HEADS:
                qk_copy(h + 1)
            for b in range(1, B):
                if h == NH * b - 5:
                    setup_mb_pe(b)
            if live:
                for t in range(1, NT):
                    act_exp(h, t)
            if 0 <= h - 3:
                dve_recip(h - 3)
            if 0 <= h - 2 < HEADS:
                dve_quant(h - 2)
            if 0 <= h - 3:
                dve_out(h - 3)
            if h % GH == 0 and h // GH < B * NG:
                dve_v_quant(h // GH)
            for b in range(1, B):
                if h == NH * b - 6:
                    setup_keep(b)
                    setup_maskc(b)
                if h == NH * b - 5:
                    setup_mb_copy(b)
            if h + GH < HEADS:
                pool_v_regroup(h // GH + 1, h % GH)
            if h % GH == 3 and h // GH + 3 < B * NG:
                load_group(h // GH + 3)
